import numpy as np
import ml_dtypes


def mxq(x, axis, fmt="e4m3"):
    dtype, down = {"e4m3": (ml_dtypes.float8_e4m3fn, 7), "e5m2": (ml_dtypes.float8_e5m2, 14)}[fmt]
    v = np.moveaxis(np.asarray(x, np.float32).astype(ml_dtypes.bfloat16).astype(np.float64), axis, -1)
    blocks = v.reshape(v.shape[:-1] + (-1, 32))
    amax = np.abs(blocks).max(-1, keepdims=True)
    byte = np.maximum(np.where(amax > 0, np.frexp(amax)[1] - 1 + 127, 0) - down, 1)
    scale = np.exp2(byte - 127.0)
    codes = (blocks / scale).astype(np.float32).astype(dtype).astype(np.float64)
    return np.moveaxis((codes * scale).reshape(v.shape), -1, axis)


WIDE = False


def mx_kscale(k):
    if not WIDE:
        return np.ones(k)
    levels = np.array([10, -10, 5, -5, 0])
    a = np.random.permutation(np.resize(levels, k // 512 * 4)).reshape(k // 512, 4)
    idx = np.arange(k)
    return np.exp2(a[idx // 512, idx % 128 // 32])


BF16 = ml_dtypes.bfloat16


def bf(x):
    return np.asarray(x, np.float32).astype(BF16)


def f64(x):
    return np.asarray(x).astype(np.float64)


E2M1 = np.array([0.0, 0.5, 1.0, 1.5, 2.0, 3.0, 4.0, 6.0, -0.0, -0.5, -1.0, -1.5, -2.0, -3.0, -4.0, -6.0])


def pack_weight(w, fmt):
    k, n = w.shape
    w = f64(bf(w)).reshape(k // 32, 32, n)
    amax = np.abs(w).max(1)
    if fmt == "e4m3":
        byte = np.frexp(amax)[1] - 1 + 127 - 7
    else:
        mant, ex = np.frexp(amax / 6.0)
        byte = np.where(mant > 0.5, ex, ex - 1) + 127
    byte = np.clip(np.where(amax > 0, byte, 1), 1, 254)
    scaled = (w * np.exp2(127.0 - byte)[:, None, :]).reshape(k, n).astype(np.float32)
    by_word = np.ascontiguousarray(scaled.reshape(k // 512, 128, 4, n).transpose(0, 1, 3, 2))
    if fmt == "e4m3":
        words = by_word.astype(ml_dtypes.float8_e4m3fn).view(np.uint8)
    else:
        c = by_word.astype(ml_dtypes.float4_e2m1fn).view(np.uint8) & 0xF
        words = c[..., 0::2] | (c[..., 1::2] << 4)
    return np.ascontiguousarray(words), np.ascontiguousarray(byte.astype(np.uint8).reshape(k // 512, 16, n))


def unpack_weight(words, scales, fmt):
    g, p, n, _ = words.shape
    if fmt == "e4m3":
        vals = np.ascontiguousarray(words).view(ml_dtypes.float8_e4m3fn).astype(np.float64)
    else:
        nib = np.empty((g, p, n, 4), np.uint8)
        nib[..., 0::2] = words & 0xF
        nib[..., 1::2] = words >> 4
        vals = E2M1[nib]
    vals = vals * np.repeat(np.exp2(scales.astype(np.float64) - 127.0), 8, axis=1)[..., None]
    return vals.transpose(0, 1, 3, 2).reshape(g * 512, n)


B, U, I, H = 4096, 4, 512, 128


def sigmoid(v):
    return 1.0 / (1.0 + np.exp(-v))


def setup_inputs():
    s = mx_kscale(I)
    inputs = bf(np.random.standard_normal((B, U, I)) * s)
    hidden = bf(np.random.standard_normal((B, U, H)))
    w_ih = np.random.standard_normal((U, 3 * H, I)) / np.sqrt(I) / s
    cat = np.ascontiguousarray(w_ih.swapaxes(1, 2)).reshape(-1, 3 * H)
    words, scales = pack_weight(cat, "e4m3")
    w_hh = bf(np.random.standard_normal((U, 3 * H, H)) / np.sqrt(H))
    b_ih = bf(np.random.standard_normal((U, 3 * H)) * 0.3)
    b_hh = bf(np.random.standard_normal((U, 3 * H)) * 0.3)
    return {"inputs": inputs,
            "hidden": hidden,
            "w_ih_words": words,
            "w_ih_scales": scales,
            "w_hh": w_hh,
            "b_ih": b_ih,
            "b_hh": b_hh}


def reference(inputs, hidden, w_ih_words, w_ih_scales, w_hh, b_ih, b_hh):
    h = f64(hidden)
    gx = (mxq(f64(inputs), 2, "e4m3").transpose(1, 0, 2) @ unpack_weight(w_ih_words, w_ih_scales, "e4m3").reshape(U, I, 3 * H)).transpose(1, 0, 2) + f64(b_ih)
    gh = (h.transpose(1, 0, 2) @ f64(w_hh).transpose(0, 2, 1)).transpose(1, 0, 2) + f64(b_hh)
    xr, xz, xn = gx[..., :H], gx[..., H:2 * H], gx[..., 2 * H:]
    hr, hz, hn = gh[..., :H], gh[..., H:2 * H], gh[..., 2 * H:]
    r = sigmoid(xr + hr)
    z = sigmoid(xz + hz)
    n = np.tanh(xn + r * hn)
    return (1.0 - z) * n + z * h

@@ -1,0 +1,368 @@
+from contextlib import ExitStack
+
+import concourse.mybir as mybir
+from concourse.masks import make_identity
+
+F32 = mybir.dt.float32
+BF16 = mybir.dt.bfloat16
+I32 = mybir.dt.int32
+U32 = mybir.dt.uint32
+U8 = mybir.dt.uint8
+FP8X4 = mybir.dt.float8_e4m3fn_x4
+ACT = mybir.ActivationFunctionType
+ALU = mybir.AluOpType
+
+BATCH, UNITS, K_IN, HID = 4096, 4, 512, 128
+P = 128
+GATES = 3
+RESET, UPDATE, NEW = 0, 1, 2
+ROW_GROUPS = 4
+CHUNK = P * ROW_GROUPS
+N_CHUNKS = (BATCH // CHUNK) * UNITS
+WORDS = K_IN // 2
+HALF = CHUNK // 2
+
+AHEAD_LOAD = 4
+AHEAD_IN = 2
+BEHIND_CAND = 1
+BEHIND_BLEND = 2
+BEHIND_OUT = 3
+
+FLOPS = 2 * BATCH * UNITS * (K_IN + HID) * GATES * HID
+
+
+def tile_grouptorchgru_t_e_kernel(
+    tc, inputs, hidden, w_ih_words, w_ih_scales, w_hh, b_ih, b_hh, out
+):
+    nc = tc.nc
+    with ExitStack() as ctx:
+        ctx.enter_context(tc.manual_schedule())
+        const = ctx.enter_context(tc.tile_pool(name="const", bufs=1))
+        x_pool = ctx.enter_context(tc.tile_pool(name="x", bufs=4))
+        hid_pool = ctx.enter_context(tc.tile_pool(name="hid", bufs=4))
+        mx_pool = ctx.enter_context(tc.tile_pool(name="mx", bufs=5))
+        ht_pool = ctx.enter_context(tc.tile_pool(name="ht", bufs=6))
+        work = ctx.enter_context(tc.tile_pool(name="work", bufs=2))
+        late = ctx.enter_context(tc.tile_pool(name="late", bufs=4))
+        mid = ctx.enter_context(tc.tile_pool(name="mid", bufs=3))
+        psum = ctx.enter_context(tc.psum_pool(name="psum", bufs=8))
+
+        x_of, hid_of, grouped_of, codes_of, planes_of, ht_of = {}, {}, {}, {}, {}, {}
+        gh_of, gx_of, pre_of, gated_of, cand_of, blend_of = {}, {}, {}, {}, {}, {}
+        xz_ps_of, xz_of, z_ps_of, reset_of, keep_of, new_of, diff_of = {}, {}, {}, {}, {}, {}, {}
+
+        def batch_rows(c):
+            first = (c // UNITS) * CHUNK
+            return slice(first, first + CHUNK)
+
+        def load(c):
+            block, u = divmod(c, UNITS)
+            x = x_pool.tile([P, ROW_GROUPS, K_IN], BF16)
+            nc.sync.dma_start(
+                out=x[:],
+                in_=inputs[batch_rows(c), u, :].rearrange("(p j) k -> p j k", j=ROW_GROUPS),
+            )
+            x_of[c] = x
+            if u == 0:
+                hid = hid_pool.tile([P, ROW_GROUPS, UNITS, HID], BF16)
+                nc.sync.dma_start(
+                    out=hid[:],
+                    in_=hidden[batch_rows(c), :, :].rearrange("(p j) u h -> p j u h", j=ROW_GROUPS),
+                )
+                hid_of[block] = hid
+
+        def transpose_inputs(c, half, copy):
+            if half == 0:
+                grouped = work.tile([P, CHUNK * 4], BF16, align_bytes=64)
+                grouped_of[c] = grouped
+            x_words = x_of[c][:].bitcast(F32)
+            grouped_words = grouped_of[c][:].bitcast(F32).rearrange("p (r w) -> p r w", w=2)
+            xt = psum.tile([P, 2, HALF], F32, tag="bank")
+            for jj in range(2):
+                for w in range(2):
+                    nc.tensor.transpose(
+                        xt[:, w, jj * P : (jj + 1) * P],
+                        x_words[:, 2 * half + jj, w:WORDS:2],
+                        ident_f32[:],
+                    )
+            copy(
+                out=grouped_words[:, half * HALF : (half + 1) * HALF, :],
+                in_=xt[:].rearrange("p w r -> p r w"),
+            )
+
+        def transpose_hidden(c, copy):
+            block, u = divmod(c, UNITS)
+            ht_ps = psum.tile([P, CHUNK], BF16, tag="bank")
+            for j in range(ROW_GROUPS):
+                nc.tensor.transpose(
+                    ht_ps[:, j * P : (j + 1) * P], hid_of[block][:, j, u, :], ident_bf[:]
+                )
+            ht = ht_pool.tile([P, CHUNK], BF16)
+            copy(out=ht[:], in_=ht_ps[:])
+            ht_of[c] = ht
+
+        def quantise(c):
+            codes = mx_pool.tile([P, CHUNK], U32, align_bytes=64)
+            planes = mx_pool.tile([P, CHUNK], U8, align_bytes=64)
+            nc.vector.quantize_mx(
+                out=codes[:].bitcast(FP8X4), scales=planes[:], in_=grouped_of[c][:]
+            )
+            codes_of[c] = codes
+            planes_of[c] = planes
+
+        def matmul_hidden(c, gate):
+            u = c % UNITS
+            gh = psum.tile([P, CHUNK], F32, tag="bank")
+            nc.tensor.matmul(
+                out=gh[:], lhsT=whh_t[:, u * GATES + gate, :], rhs=ht_of[c][:], start=True, stop=True
+            )
+            gh_of[c, gate] = gh
+
+        def matmul_inputs(c, gate):
+            u = c % UNITS
+            cols = slice(gate * HID, (gate + 1) * HID)
+            gx = psum.tile([P, CHUNK], F32, tag="bank")
+            nc.tensor.matmul_mx(
+                out=gx[:],
+                lhsT=w_words[:, u, cols].bitcast(FP8X4),
+                lhsT_scale=w_planes[:, u, cols],
+                rhs=codes_of[c][:].bitcast(FP8X4),
+                rhs_scale=planes_of[c][:],
+                start=True,
+                stop=True,
+            )
+            gx_of[c, gate] = gx
+
+        def matmul_inputs_update(c):
+            u = c % UNITS
+            cols = slice(UPDATE * HID, (UPDATE + 1) * HID)
+            xz_ps = psum.tile([P, ROW_GROUPS, HID], F32, tag="bank")
+            for j in range(ROW_GROUPS):
+                rows = slice(j * P, (j + 1) * P)
+                nc.tensor.matmul_mx(
+                    out=xz_ps[:, j, :],
+                    lhsT=codes_of[c][:, rows].bitcast(FP8X4),
+                    lhsT_scale=planes_of[c][:, rows],
+                    rhs=w_words[:, u, cols].bitcast(FP8X4),
+                    rhs_scale=w_planes[:, u, cols],
+                    start=True,
+                    stop=True,
+                )
+            xz_ps_of[c] = xz_ps
+
+        def copy_inputs_update(c):
+            xz = mid.tile([P, ROW_GROUPS, HID], F32)
+            nc.scalar.copy(out=xz[:], in_=xz_ps_of[c][:])
+            xz_of[c] = xz
+
+        def sum_update(c):
+            u = c % UNITS
+            z_ps = psum.tile([P, CHUNK], F32, tag="bank")
+            nc.tensor.matmul(
+                out=z_ps[:], lhsT=whh_t[:, u * GATES + UPDATE, :], rhs=ht_of[c][:],
+                start=True, stop=False,
+            )
+            for j in range(ROW_GROUPS):
+                nc.tensor.matmul(
+                    out=z_ps[:, j * P : (j + 1) * P], lhsT=xz_of[c][:, j, :], rhs=ident_f32[:],
+                    is_transpose=True, start=False, stop=(j == ROW_GROUPS - 1),
+                )
+            z_ps_of[c] = z_ps
+
+        def sigmoid_update(c):
+            z_col = (c % UNITS) * GATES + UPDATE
+            keep = late.tile([P, CHUNK], F32)
+            nc.scalar.activation(
+                out=keep[:], in_=z_ps_of[c][:], func=ACT.Sigmoid,
+                bias=bias_neg[:, z_col : z_col + 1], scale=-1.0,
+            )
+            keep_of[c] = keep
+
+        def copy_hidden_reset(c):
+            r_col = (c % UNITS) * GATES + RESET
+            pre = work.tile([P, CHUNK], F32)
+            nc.scalar.activation(
+                out=pre[:], in_=gh_of[c, RESET][:], func=ACT.Identity,
+                bias=bias_sum[:, r_col : r_col + 1], scale=1.0,
+            )
+            pre_of[c] = pre
+
+        def sum_reset(c):
+            nc.vector.tensor_tensor(
+                out=pre_of[c][:], in0=pre_of[c][:], in1=gx_of[c, RESET][:], op=ALU.add
+            )
+
+        def sigmoid_reset(c):
+            reset = mid.tile([P, CHUNK], F32)
+            nc.scalar.activation(out=reset[:], in_=pre_of[c][:], func=ACT.Sigmoid)
+            reset_of[c] = reset
+
+        def gate_hidden(c):
+            n_col = (c % UNITS) * GATES + NEW
+            gated = work.tile([P, CHUNK], F32)
+            nc.vector.scalar_tensor_tensor(
+                out=gated[:], in0=gh_of[c, NEW][:], scalar=bias_hh[:, n_col : n_col + 1],
+                in1=reset_of[c][:], op0=ALU.add, op1=ALU.mult,
+            )
+            gated_of[c] = gated
+
+        def sum_candidate(c):
+            cand = work.tile([P, CHUNK], F32)
+            nc.vector.tensor_tensor(
+                out=cand[:], in0=gated_of[c][:], in1=gx_of[c, NEW][:], op=ALU.add
+            )
+            cand_of[c] = cand
+
+        def on_gpsimd(c):
+            return c < N_CHUNKS - 2
+
+        def blend_engine(c):
+            return nc.gpsimd if on_gpsimd(c) else nc.vector
+
+        def candidate(c):
+            n_col = (c % UNITS) * GATES + NEW
+            new = work.tile([P, CHUNK], F32)
+            nc.scalar.activation(
+                out=new[:], in_=cand_of[c][:], func=ACT.Tanh,
+                bias=bias_ih[:, n_col : n_col + 1], scale=1.0,
+            )
+            new_of[c] = new
+
+        def difference(c):
+            diff = work.tile([P, CHUNK], F32)
+            blend_engine(c).tensor_tensor(
+                out=diff[:], in0=new_of[c][:], in1=ht_of[c][:], op=ALU.subtract
+            )
+            diff_of[c] = diff
+
+        def blend(c):
+            mixed = late.tile([P, CHUNK], F32)
+            blend_engine(c).tensor_tensor(out=mixed[:], in0=keep_of[c][:], in1=diff_of[c][:], op=ALU.mult)
+            blend_of[c] = mixed
+
+        def transpose_out(c):
+            block, u = divmod(c, UNITS)
+            back = psum.tile([P, ROW_GROUPS, HID], F32, tag="bank")
+            for j in range(ROW_GROUPS):
+                nc.tensor.transpose(
+                    back[:, j, :], blend_of[c][:, j * P : (j + 1) * P], ident_f32[:]
+                )
+            result = late.tile([P, ROW_GROUPS, HID], F32)
+            nc.vector.tensor_tensor(
+                out=result[:], in0=back[:], in1=hid_of[block][:, :, u, :], op=ALU.add
+            )
+            nc.sync.dma_start(
+                out=out[batch_rows(c), u, :].rearrange("(p j) h -> p j h", j=ROW_GROUPS),
+                in_=result[:],
+            )
+
+        def run(stage, c, *args):
+            if 0 <= c < N_CHUNKS:
+                stage(c, *args)
+
+        warm = const.tile([P, 1], F32)
+        nc.vector.memset(warm[:], 0.0)
+        nc.scalar.activation(out=warm[:], in_=warm[:], func=ACT.Sigmoid)
+
+        ident_f32 = const.tile([P, P], F32)
+        make_identity(nc, ident_f32[:])
+        ident_bf = const.tile([P, P], BF16)
+        make_identity(nc, ident_bf[:])
+
+        w_planes = const.tile([P, UNITS, GATES * HID], U8, align_bytes=64)
+        nc.vector.memset(w_planes[:].bitcast(I32), 0)
+        bias_rows = const.tile([P, P], BF16)
+        nc.vector.memset(bias_rows[:], 0.0)
+
+        load(0)
+        whh_rows = const.tile([P, UNITS * GATES, HID], BF16)
+        nc.sync.dma_start(out=whh_rows[:], in_=w_hh.rearrange("u (g m) k -> m (u g) k", m=P))
+        n_bias = UNITS * GATES
+        nc.sync.dma_start(out=bias_rows[0:n_bias, :], in_=b_ih.rearrange("u (g h) -> (u g) h", h=HID))
+        nc.sync.dma_start(
+            out=bias_rows[n_bias : 2 * n_bias, :], in_=b_hh.rearrange("u (g h) -> (u g) h", h=HID)
+        )
+        for quadrant in range(4):
+            nc.sync.dma_start(
+                out=w_planes[32 * quadrant : 32 * quadrant + 4, :, :].bitcast(I32),
+                in_=w_ih_scales[:, 4 * quadrant : 4 * quadrant + 4, :]
+                .rearrange("u q n -> q u n")
+                .bitcast(I32),
+            )
+        w_words = const.tile([P, UNITS, GATES * HID], U32, align_bytes=64)
+
+        def load_words(u):
+            nc.sync.dma_start(
+                out=w_words[:, u, :].bitcast(I32),
+                in_=w_ih_words[u].rearrange("p n t -> p (n t)").bitcast(I32),
+            )
+
+        load_words(0)
+        load(1)
+        load(2)
+        for u in range(1, UNITS):
+            load_words(u)
+        load(3)
+
+        transpose_inputs(0, 0, nc.scalar.copy)
+        transpose_hidden(0, nc.scalar.copy)
+        transpose_inputs(0, 1, nc.vector.tensor_copy)
+        quantise(0)
+
+        whh_t = const.tile([P, UNITS * GATES, P], BF16)
+        bias_ih = const.tile([P, n_bias], F32)
+        bias_hh = const.tile([P, n_bias], F32)
+        bias_sum = const.tile([P, n_bias], F32)
+        bias_neg = const.tile([P, n_bias], F32)
+
+        def prepare_weights():
+            for u in range(UNITS):
+                whh_ps = psum.tile([P, GATES, P], BF16, tag="bank")
+                for gate in range(GATES):
+                    nc.tensor.transpose(
+                        whh_ps[:, gate, :], whh_rows[:, u * GATES + gate, :], ident_bf[:]
+                    )
+                nc.vector.tensor_copy(out=whh_t[:, u * GATES : (u + 1) * GATES, :], in_=whh_ps[:])
+            bias_ps = psum.tile([P, P], BF16, tag="bank")
+            nc.tensor.transpose(bias_ps[:], bias_rows[:], ident_bf[:])
+            nc.vector.tensor_copy(out=bias_ih[:], in_=bias_ps[:, 0:n_bias])
+            nc.vector.tensor_copy(out=bias_hh[:], in_=bias_ps[:, n_bias : 2 * n_bias])
+            nc.vector.tensor_tensor(out=bias_sum[:], in0=bias_ih[:], in1=bias_hh[:], op=ALU.add)
+            nc.vector.tensor_scalar_mul(out=bias_neg[:], in0=bias_sum[:], scalar1=-1.0)
+
+        prepare_weights()
+        for i in range(N_CHUNKS + BEHIND_OUT):
+            run(load, i + AHEAD_LOAD)
+            run(matmul_hidden, i, RESET)
+            run(matmul_inputs, i, RESET)
+            run(matmul_inputs_update, i)
+            run(matmul_inputs, i - BEHIND_CAND, NEW)
+            run(matmul_hidden, i - BEHIND_CAND, NEW)
+            run(copy_hidden_reset, i)
+            run(candidate, i - BEHIND_BLEND)
+            if on_gpsimd(i - BEHIND_BLEND):
+                run(difference, i - BEHIND_BLEND)
+            run(sum_reset, i)
+            run(copy_inputs_update, i)
+            run(gate_hidden, i - BEHIND_CAND)
+            if not on_gpsimd(i - BEHIND_BLEND):
+                run(difference, i - BEHIND_BLEND)
+            if i == 0:
+                transpose_inputs(1, 0, nc.scalar.copy)
+                transpose_inputs(1, 1, nc.vector.tensor_copy)
+                transpose_hidden(1, nc.scalar.copy)
+            run(transpose_inputs, i + AHEAD_IN, 0, nc.scalar.copy)
+            run(transpose_hidden, i + AHEAD_IN, nc.vector.tensor_copy)
+            run(sum_candidate, i - BEHIND_CAND)
+            run(sigmoid_reset, i)
+            run(sum_update, i - BEHIND_CAND)
+            run(sigmoid_update, i - BEHIND_CAND)
+            run(transpose_inputs, i + AHEAD_IN, 1, nc.vector.tensor_copy)
+            if i == 0:
+                quantise(1)
+            if not on_gpsimd(i - BEHIND_BLEND):
+                run(blend, i - BEHIND_BLEND)
+            run(transpose_out, i - BEHIND_OUT)
+            run(quantise, i + AHEAD_IN)
+            if on_gpsimd(i - BEHIND_BLEND):
+                run(blend, i - BEHIND_BLEND)

@@ -16,17 +16,18 @@ BATCH, UNITS, K_IN, HID = 4096, 4, 512, 128
 P = 128
 GATES = 3
 RESET, UPDATE, NEW = 0, 1, 2
-ROW_GROUPS = 4
-CHUNK = P * ROW_GROUPS
-N_CHUNKS = (BATCH // CHUNK) * UNITS
+CHUNK = 512
+SHORT = CHUNK // 2
+LAST = (BATCH // CHUNK) * UNITS
+N_CHUNKS = LAST + 1
 WORDS = K_IN // 2
-HALF = CHUNK // 2
 
 AHEAD_LOAD = 4
 AHEAD_IN = 2
 BEHIND_CAND = 1
 BEHIND_BLEND = 2
 BEHIND_OUT = 3
+BLEND_ON_VECTOR = 2
 
 FLOPS = 2 * BATCH * UNITS * (K_IN + HID) * GATES * HID
 
@@ -47,63 +48,87 @@ def tile_grouptorchgru_t_e_kernel(
         mid = ctx.enter_context(tc.tile_pool(name="mid", bufs=3))
         psum = ctx.enter_context(tc.psum_pool(name="psum", bufs=8))
 
-        x_of, hid_of, grouped_of, codes_of, planes_of, ht_of = {}, {}, {}, {}, {}, {}
-        gh_of, gx_of, pre_of, gated_of, cand_of, blend_of = {}, {}, {}, {}, {}, {}
-        xz_ps_of, xz_of, z_ps_of, reset_of, keep_of, new_of, diff_of = {}, {}, {}, {}, {}, {}, {}
+        x_of, hid_of, xt_of, grouped_of, codes_of, planes_of = {}, {}, {}, {}, {}, {}
+        ht_ps_of, ht_of, gh_of, gx_of, xz_ps_of, xz_of, z_ps_of = {}, {}, {}, {}, {}, {}, {}
+        pre_of, reset_of, keep_of, gated_of, cand_of = {}, {}, {}, {}, {}
+        new_of, diff_of, blend_of, back_of = {}, {}, {}, {}
+
+        def unit(c):
+            return c % UNITS
+
+        def rows(c):
+            return SHORT if c in (0, LAST) else CHUNK
+
+        def groups(c):
+            return rows(c) // P
 
         def batch_rows(c):
-            first = (c // UNITS) * CHUNK
-            return slice(first, first + CHUNK)
+            first = SHORT if c == LAST else (c // UNITS) * CHUNK
+            return slice(first, first + rows(c))
 
         def load(c):
-            block, u = divmod(c, UNITS)
-            x = x_pool.tile([P, ROW_GROUPS, K_IN], BF16)
+            x = x_pool.tile([P, groups(c), K_IN], BF16)
             nc.sync.dma_start(
                 out=x[:],
-                in_=inputs[batch_rows(c), u, :].rearrange("(p j) k -> p j k", j=ROW_GROUPS),
+                in_=inputs[batch_rows(c), unit(c), :].rearrange("(p j) k -> p j k", j=groups(c)),
             )
             x_of[c] = x
-            if u == 0:
-                hid = hid_pool.tile([P, ROW_GROUPS, UNITS, HID], BF16)
+            if c in (0, LAST):
+                units = slice(0, 1)
+            elif c == 1:
+                units = slice(1, UNITS)
+            elif unit(c) == 0:
+                units = slice(0, UNITS)
+            else:
+                units = slice(0, 0)
+            count = units.stop - units.start
+            if count > 0:
+                hid = hid_pool.tile([P, groups(c), count, HID], BF16)
                 nc.sync.dma_start(
                     out=hid[:],
-                    in_=hidden[batch_rows(c), :, :].rearrange("(p j) u h -> p j u h", j=ROW_GROUPS),
+                    in_=hidden[batch_rows(c), units, :].rearrange("(p j) u h -> p j u h", j=groups(c)),
                 )
-                hid_of[block] = hid
+                for k in range(count):
+                    hid_of[c + k] = hid[:, :, k, :]
 
-        def transpose_inputs(c, half, copy):
-            if half == 0:
-                grouped = work.tile([P, CHUNK * 4], BF16, align_bytes=64)
-                grouped_of[c] = grouped
+        def transpose_inputs(c, half):
+            n = groups(c) // 2
+            xt = psum.tile([P, 2, n * P], F32, tag="bank")
             x_words = x_of[c][:].bitcast(F32)
-            grouped_words = grouped_of[c][:].bitcast(F32).rearrange("p (r w) -> p r w", w=2)
-            xt = psum.tile([P, 2, HALF], F32, tag="bank")
-            for jj in range(2):
+            for jj in range(n):
                 for w in range(2):
                     nc.tensor.transpose(
                         xt[:, w, jj * P : (jj + 1) * P],
-                        x_words[:, 2 * half + jj, w:WORDS:2],
+                        x_words[:, n * half + jj, w:WORDS:2],
                         ident_f32[:],
                     )
+            xt_of[c, half] = xt
+
+        def copy_inputs(c, half, copy):
+            if half == 0:
+                grouped = work.tile([P, rows(c) * 4], BF16, align_bytes=64)
+                grouped_of[c] = grouped
+            grouped_words = grouped_of[c][:].bitcast(F32).rearrange("p (r w) -> p r w", w=2)
+            n = rows(c) // 2
             copy(
-                out=grouped_words[:, half * HALF : (half + 1) * HALF, :],
-                in_=xt[:].rearrange("p w r -> p r w"),
+                out=grouped_words[:, half * n : (half + 1) * n, :],
+                in_=xt_of[c, half][:].rearrange("p w r -> p r w"),
             )
 
-        def transpose_hidden(c, copy):
-            block, u = divmod(c, UNITS)
-            ht_ps = psum.tile([P, CHUNK], BF16, tag="bank")
-            for j in range(ROW_GROUPS):
-                nc.tensor.transpose(
-                    ht_ps[:, j * P : (j + 1) * P], hid_of[block][:, j, u, :], ident_bf[:]
-                )
-            ht = ht_pool.tile([P, CHUNK], BF16)
-            copy(out=ht[:], in_=ht_ps[:])
+        def transpose_hidden(c):
+            ht_ps = psum.tile([P, rows(c)], BF16, tag="bank")
+            for j in range(groups(c)):
+                nc.tensor.transpose(ht_ps[:, j * P : (j + 1) * P], hid_of[c][:, j, :], ident_bf[:])
+            ht_ps_of[c] = ht_ps
+
+        def copy_hidden(c, copy):
+            ht = ht_pool.tile([P, rows(c)], BF16)
+            copy(out=ht[:], in_=ht_ps_of[c][:])
             ht_of[c] = ht
 
         def quantise(c):
-            codes = mx_pool.tile([P, CHUNK], U32, align_bytes=64)
-            planes = mx_pool.tile([P, CHUNK], U8, align_bytes=64)
+            codes = mx_pool.tile([P, rows(c)], U32, align_bytes=64)
+            planes = mx_pool.tile([P, rows(c)], U8, align_bytes=64)
             nc.vector.quantize_mx(
                 out=codes[:].bitcast(FP8X4), scales=planes[:], in_=grouped_of[c][:]
             )
@@ -111,21 +136,20 @@ def tile_grouptorchgru_t_e_kernel(
             planes_of[c] = planes
 
         def matmul_hidden(c, gate):
-            u = c % UNITS
-            gh = psum.tile([P, CHUNK], F32, tag="bank")
+            gh = psum.tile([P, rows(c)], F32, tag="bank")
             nc.tensor.matmul(
-                out=gh[:], lhsT=whh_t[:, u * GATES + gate, :], rhs=ht_of[c][:], start=True, stop=True
+                out=gh[:], lhsT=whh_t[:, unit(c) * GATES + gate, :], rhs=ht_of[c][:],
+                start=True, stop=True,
             )
             gh_of[c, gate] = gh
 
         def matmul_inputs(c, gate):
-            u = c % UNITS
             cols = slice(gate * HID, (gate + 1) * HID)
-            gx = psum.tile([P, CHUNK], F32, tag="bank")
+            gx = psum.tile([P, rows(c)], F32, tag="bank")
             nc.tensor.matmul_mx(
                 out=gx[:],
-                lhsT=w_words[:, u, cols].bitcast(FP8X4),
-                lhsT_scale=w_planes[:, u, cols],
+                lhsT=w_words[:, unit(c), cols].bitcast(FP8X4),
+                lhsT_scale=w_planes[:, unit(c), cols],
                 rhs=codes_of[c][:].bitcast(FP8X4),
                 rhs_scale=planes_of[c][:],
                 start=True,
@@ -134,44 +158,42 @@ def tile_grouptorchgru_t_e_kernel(
             gx_of[c, gate] = gx
 
         def matmul_inputs_update(c):
-            u = c % UNITS
             cols = slice(UPDATE * HID, (UPDATE + 1) * HID)
-            xz_ps = psum.tile([P, ROW_GROUPS, HID], F32, tag="bank")
-            for j in range(ROW_GROUPS):
-                rows = slice(j * P, (j + 1) * P)
+            xz_ps = psum.tile([P, groups(c), HID], F32, tag="bank")
+            for j in range(groups(c)):
+                part = slice(j * P, (j + 1) * P)
                 nc.tensor.matmul_mx(
                     out=xz_ps[:, j, :],
-                    lhsT=codes_of[c][:, rows].bitcast(FP8X4),
-                    lhsT_scale=planes_of[c][:, rows],
-                    rhs=w_words[:, u, cols].bitcast(FP8X4),
-                    rhs_scale=w_planes[:, u, cols],
+                    lhsT=codes_of[c][:, part].bitcast(FP8X4),
+                    lhsT_scale=planes_of[c][:, part],
+                    rhs=w_words[:, unit(c), cols].bitcast(FP8X4),
+                    rhs_scale=w_planes[:, unit(c), cols],
                     start=True,
                     stop=True,
                 )
             xz_ps_of[c] = xz_ps
 
         def copy_inputs_update(c):
-            xz = mid.tile([P, ROW_GROUPS, HID], F32)
+            xz = mid.tile([P, groups(c), HID], F32)
             nc.scalar.copy(out=xz[:], in_=xz_ps_of[c][:])
             xz_of[c] = xz
 
         def sum_update(c):
-            u = c % UNITS
-            z_ps = psum.tile([P, CHUNK], F32, tag="bank")
+            z_ps = psum.tile([P, rows(c)], F32, tag="bank")
             nc.tensor.matmul(
-                out=z_ps[:], lhsT=whh_t[:, u * GATES + UPDATE, :], rhs=ht_of[c][:],
+                out=z_ps[:], lhsT=whh_t[:, unit(c) * GATES + UPDATE, :], rhs=ht_of[c][:],
                 start=True, stop=False,
             )
-            for j in range(ROW_GROUPS):
+            for j in range(groups(c)):
                 nc.tensor.matmul(
                     out=z_ps[:, j * P : (j + 1) * P], lhsT=xz_of[c][:, j, :], rhs=ident_f32[:],
-                    is_transpose=True, start=False, stop=(j == ROW_GROUPS - 1),
+                    is_transpose=True, start=False, stop=(j == groups(c) - 1),
                 )
             z_ps_of[c] = z_ps
 
         def sigmoid_update(c):
-            z_col = (c % UNITS) * GATES + UPDATE
-            keep = late.tile([P, CHUNK], F32)
+            z_col = unit(c) * GATES + UPDATE
+            keep = late.tile([P, rows(c)], F32)
             nc.scalar.activation(
                 out=keep[:], in_=z_ps_of[c][:], func=ACT.Sigmoid,
                 bias=bias_neg[:, z_col : z_col + 1], scale=-1.0,
@@ -179,8 +201,8 @@ def tile_grouptorchgru_t_e_kernel(
             keep_of[c] = keep
 
         def copy_hidden_reset(c):
-            r_col = (c % UNITS) * GATES + RESET
-            pre = work.tile([P, CHUNK], F32)
+            r_col = unit(c) * GATES + RESET
+            pre = work.tile([P, rows(c)], F32)
             nc.scalar.activation(
                 out=pre[:], in_=gh_of[c, RESET][:], func=ACT.Identity,
                 bias=bias_sum[:, r_col : r_col + 1], scale=1.0,
@@ -193,13 +215,13 @@ def tile_grouptorchgru_t_e_kernel(
             )
 
         def sigmoid_reset(c):
-            reset = mid.tile([P, CHUNK], F32)
+            reset = mid.tile([P, rows(c)], F32)
             nc.scalar.activation(out=reset[:], in_=pre_of[c][:], func=ACT.Sigmoid)
             reset_of[c] = reset
 
         def gate_hidden(c):
-            n_col = (c % UNITS) * GATES + NEW
-            gated = work.tile([P, CHUNK], F32)
+            n_col = unit(c) * GATES + NEW
+            gated = work.tile([P, rows(c)], F32)
             nc.vector.scalar_tensor_tensor(
                 out=gated[:], in0=gh_of[c, NEW][:], scalar=bias_hh[:, n_col : n_col + 1],
                 in1=reset_of[c][:], op0=ALU.add, op1=ALU.mult,
@@ -207,21 +229,21 @@ def tile_grouptorchgru_t_e_kernel(
             gated_of[c] = gated
 
         def sum_candidate(c):
-            cand = work.tile([P, CHUNK], F32)
+            cand = work.tile([P, rows(c)], F32)
             nc.vector.tensor_tensor(
                 out=cand[:], in0=gated_of[c][:], in1=gx_of[c, NEW][:], op=ALU.add
             )
             cand_of[c] = cand
 
         def on_gpsimd(c):
-            return c < N_CHUNKS - 2
+            return c < N_CHUNKS - BLEND_ON_VECTOR
 
         def blend_engine(c):
             return nc.gpsimd if on_gpsimd(c) else nc.vector
 
         def candidate(c):
-            n_col = (c % UNITS) * GATES + NEW
-            new = work.tile([P, CHUNK], F32)
+            n_col = unit(c) * GATES + NEW
+            new = work.tile([P, rows(c)], F32)
             nc.scalar.activation(
                 out=new[:], in_=cand_of[c][:], func=ACT.Tanh,
                 bias=bias_ih[:, n_col : n_col + 1], scale=1.0,
@@ -229,30 +251,28 @@ def tile_grouptorchgru_t_e_kernel(
             new_of[c] = new
 
         def difference(c):
-            diff = work.tile([P, CHUNK], F32)
+            diff = work.tile([P, rows(c)], F32)
             blend_engine(c).tensor_tensor(
                 out=diff[:], in0=new_of[c][:], in1=ht_of[c][:], op=ALU.subtract
             )
             diff_of[c] = diff
 
         def blend(c):
-            mixed = late.tile([P, CHUNK], F32)
+            mixed = late.tile([P, rows(c)], F32)
             blend_engine(c).tensor_tensor(out=mixed[:], in0=keep_of[c][:], in1=diff_of[c][:], op=ALU.mult)
             blend_of[c] = mixed
 
         def transpose_out(c):
-            block, u = divmod(c, UNITS)
-            back = psum.tile([P, ROW_GROUPS, HID], F32, tag="bank")
-            for j in range(ROW_GROUPS):
-                nc.tensor.transpose(
-                    back[:, j, :], blend_of[c][:, j * P : (j + 1) * P], ident_f32[:]
-                )
-            result = late.tile([P, ROW_GROUPS, HID], F32)
-            nc.vector.tensor_tensor(
-                out=result[:], in0=back[:], in1=hid_of[block][:, :, u, :], op=ALU.add
-            )
+            back = psum.tile([P, groups(c), HID], F32, tag="bank")
+            for j in range(groups(c)):
+                nc.tensor.transpose(back[:, j, :], blend_of[c][:, j * P : (j + 1) * P], ident_f32[:])
+            back_of[c] = back
+
+        def store(c):
+            result = late.tile([P, groups(c), HID], F32)
+            nc.vector.tensor_tensor(out=result[:], in0=back_of[c][:], in1=hid_of[c], op=ALU.add)
             nc.sync.dma_start(
-                out=out[batch_rows(c), u, :].rearrange("(p j) h -> p j h", j=ROW_GROUPS),
+                out=out[batch_rows(c), unit(c), :].rearrange("(p j) h -> p j h", j=groups(c)),
                 in_=result[:],
             )
 
@@ -304,9 +324,12 @@ def tile_grouptorchgru_t_e_kernel(
             load_words(u)
         load(3)
 
-        transpose_inputs(0, 0, nc.scalar.copy)
-        transpose_hidden(0, nc.scalar.copy)
-        transpose_inputs(0, 1, nc.vector.tensor_copy)
+        transpose_inputs(0, 0)
+        copy_inputs(0, 0, nc.scalar.copy)
+        transpose_inputs(0, 1)
+        copy_inputs(0, 1, nc.vector.tensor_copy)
+        transpose_hidden(0)
+        copy_hidden(0, nc.scalar.copy)
         quantise(0)
 
         whh_t = const.tile([P, UNITS * GATES, P], BF16)
@@ -315,54 +338,58 @@ def tile_grouptorchgru_t_e_kernel(
         bias_sum = const.tile([P, n_bias], F32)
         bias_neg = const.tile([P, n_bias], F32)
 
-        def prepare_weights():
-            for u in range(UNITS):
-                whh_ps = psum.tile([P, GATES, P], BF16, tag="bank")
-                for gate in range(GATES):
-                    nc.tensor.transpose(
-                        whh_ps[:, gate, :], whh_rows[:, u * GATES + gate, :], ident_bf[:]
-                    )
-                nc.vector.tensor_copy(out=whh_t[:, u * GATES : (u + 1) * GATES, :], in_=whh_ps[:])
-            bias_ps = psum.tile([P, P], BF16, tag="bank")
-            nc.tensor.transpose(bias_ps[:], bias_rows[:], ident_bf[:])
-            nc.vector.tensor_copy(out=bias_ih[:], in_=bias_ps[:, 0:n_bias])
-            nc.vector.tensor_copy(out=bias_hh[:], in_=bias_ps[:, n_bias : 2 * n_bias])
-            nc.vector.tensor_tensor(out=bias_sum[:], in0=bias_ih[:], in1=bias_hh[:], op=ALU.add)
-            nc.vector.tensor_scalar_mul(out=bias_neg[:], in0=bias_sum[:], scalar1=-1.0)
+        bias_ps = psum.tile([P, P], BF16, tag="bank")
+        nc.tensor.transpose(bias_ps[:], bias_rows[:], ident_bf[:])
+        nc.vector.tensor_copy(out=bias_ih[:], in_=bias_ps[:, 0:n_bias])
+        nc.vector.tensor_copy(out=bias_hh[:], in_=bias_ps[:, n_bias : 2 * n_bias])
+        nc.vector.tensor_tensor(out=bias_sum[:], in0=bias_ih[:], in1=bias_hh[:], op=ALU.add)
+        nc.vector.tensor_scalar_mul(out=bias_neg[:], in0=bias_sum[:], scalar1=-1.0)
+        for u in range(UNITS):
+            whh_ps = psum.tile([P, GATES, P], BF16, tag="bank")
+            for gate in range(GATES):
+                nc.tensor.transpose(
+                    whh_ps[:, gate, :], whh_rows[:, u * GATES + gate, :], ident_bf[:]
+                )
+            nc.scalar.copy(out=whh_t[:, u * GATES : (u + 1) * GATES, :], in_=whh_ps[:])
 
-        prepare_weights()
         for i in range(N_CHUNKS + BEHIND_OUT):
+            cand, ahead = i - BEHIND_CAND, i + AHEAD_IN
             run(load, i + AHEAD_LOAD)
             run(matmul_hidden, i, RESET)
-            run(matmul_inputs, i, RESET)
-            run(matmul_inputs_update, i)
-            run(matmul_inputs, i - BEHIND_CAND, NEW)
-            run(matmul_hidden, i - BEHIND_CAND, NEW)
             run(copy_hidden_reset, i)
             run(candidate, i - BEHIND_BLEND)
             if on_gpsimd(i - BEHIND_BLEND):
                 run(difference, i - BEHIND_BLEND)
+            if on_gpsimd(i - BEHIND_BLEND):
+                run(blend, i - BEHIND_BLEND)
+            run(matmul_inputs, i, RESET)
             run(sum_reset, i)
+            run(matmul_inputs_update, i)
             run(copy_inputs_update, i)
-            run(gate_hidden, i - BEHIND_CAND)
+            run(matmul_inputs, cand, NEW)
+            run(matmul_hidden, cand, NEW)
+            run(gate_hidden, cand)
             if not on_gpsimd(i - BEHIND_BLEND):
                 run(difference, i - BEHIND_BLEND)
             if i == 0:
-                transpose_inputs(1, 0, nc.scalar.copy)
-                transpose_inputs(1, 1, nc.vector.tensor_copy)
-                transpose_hidden(1, nc.scalar.copy)
-            run(transpose_inputs, i + AHEAD_IN, 0, nc.scalar.copy)
-            run(transpose_hidden, i + AHEAD_IN, nc.vector.tensor_copy)
-            run(sum_candidate, i - BEHIND_CAND)
-            run(sigmoid_reset, i)
-            run(sum_update, i - BEHIND_CAND)
-            run(sigmoid_update, i - BEHIND_CAND)
-            run(transpose_inputs, i + AHEAD_IN, 1, nc.vector.tensor_copy)
-            if i == 0:
+                for half, copy in ((0, nc.scalar.copy), (1, nc.vector.tensor_copy)):
+                    transpose_inputs(1, half)
+                    copy_inputs(1, half, copy)
+                transpose_hidden(1)
+                copy_hidden(1, nc.scalar.copy)
                 quantise(1)
+            run(transpose_inputs, ahead, 0)
+            run(copy_inputs, ahead, 0, nc.scalar.copy)
+            run(sigmoid_reset, i)
+            run(transpose_hidden, ahead)
+            run(copy_hidden, ahead, nc.vector.tensor_copy)
+            run(sum_candidate, cand)
+            run(sum_update, cand)
+            run(sigmoid_update, cand)
+            run(transpose_inputs, ahead, 1)
+            run(copy_inputs, ahead, 1, nc.vector.tensor_copy)
             if not on_gpsimd(i - BEHIND_BLEND):
                 run(blend, i - BEHIND_BLEND)
             run(transpose_out, i - BEHIND_OUT)
-            run(quantise, i + AHEAD_IN)
-            if on_gpsimd(i - BEHIND_BLEND):
-                run(blend, i - BEHIND_BLEND)
+            run(store, i - BEHIND_OUT)
+            run(quantise, ahead)

@@ -66,13 +66,19 @@ def tile_grouptorchgru_t_e_kernel(
             first = SHORT if c == LAST else (c // UNITS) * CHUNK
             return slice(first, first + rows(c))
 
-        def load(c):
+        def column(bias, c, gate):
+            u = unit(c)
+            return bias[:, gate, u : u + 1]
+
+        def load_inputs(c):
             x = x_pool.tile([P, groups(c), K_IN], BF16)
             nc.sync.dma_start(
                 out=x[:],
                 in_=inputs[batch_rows(c), unit(c), :].rearrange("(p j) k -> p j k", j=groups(c)),
             )
             x_of[c] = x
+
+        def load_hidden(c):
             if c in (0, LAST):
                 units = slice(0, 1)
             elif c == 1:
@@ -90,6 +96,10 @@ def tile_grouptorchgru_t_e_kernel(
                 )
                 for k in range(count):
                     hid_of[c + k] = hid[:, :, k, :]
+
+        def load(c):
+            load_inputs(c)
+            load_hidden(c)
 
         def transpose_inputs(c, half):
             n = groups(c) // 2
@@ -192,20 +202,18 @@ def tile_grouptorchgru_t_e_kernel(
             z_ps_of[c] = z_ps
 
         def sigmoid_update(c):
-            z_col = unit(c) * GATES + UPDATE
             keep = late.tile([P, rows(c)], F32)
             nc.scalar.activation(
                 out=keep[:], in_=z_ps_of[c][:], func=ACT.Sigmoid,
-                bias=bias_neg[:, z_col : z_col + 1], scale=-1.0,
+                bias=column(bias_neg, c, UPDATE), scale=-1.0,
             )
             keep_of[c] = keep
 
         def copy_hidden_reset(c):
-            r_col = unit(c) * GATES + RESET
             pre = work.tile([P, rows(c)], F32)
             nc.scalar.activation(
                 out=pre[:], in_=gh_of[c, RESET][:], func=ACT.Identity,
-                bias=bias_sum[:, r_col : r_col + 1], scale=1.0,
+                bias=column(bias_sum, c, RESET), scale=1.0,
             )
             pre_of[c] = pre
 
@@ -220,10 +228,9 @@ def tile_grouptorchgru_t_e_kernel(
             reset_of[c] = reset
 
         def gate_hidden(c):
-            n_col = unit(c) * GATES + NEW
             gated = work.tile([P, rows(c)], F32)
             nc.vector.scalar_tensor_tensor(
-                out=gated[:], in0=gh_of[c, NEW][:], scalar=bias_hh[:, n_col : n_col + 1],
+                out=gated[:], in0=gh_of[c, NEW][:], scalar=column(bias_hh, c, NEW),
                 in1=reset_of[c][:], op0=ALU.add, op1=ALU.mult,
             )
             gated_of[c] = gated
@@ -242,11 +249,10 @@ def tile_grouptorchgru_t_e_kernel(
             return nc.gpsimd if on_gpsimd(c) else nc.vector
 
         def candidate(c):
-            n_col = unit(c) * GATES + NEW
             new = work.tile([P, rows(c)], F32)
             nc.scalar.activation(
                 out=new[:], in_=cand_of[c][:], func=ACT.Tanh,
-                bias=bias_ih[:, n_col : n_col + 1], scale=1.0,
+                bias=column(bias_ih, c, NEW), scale=1.0,
             )
             new_of[c] = new
 
@@ -280,6 +286,10 @@ def tile_grouptorchgru_t_e_kernel(
             if 0 <= c < N_CHUNKS:
                 stage(c, *args)
 
+        w_planes = const.tile([P, UNITS, GATES * HID], U8, align_bytes=64)
+        nc.vector.memset(w_planes[:].bitcast(I32), 0)
+        bias_rows = const.tile([P, GATES * HID], BF16)
+        nc.vector.memset(bias_rows[:], 0.0)
         warm = const.tile([P, 1], F32)
         nc.vector.memset(warm[:], 0.0)
         nc.scalar.activation(out=warm[:], in_=warm[:], func=ACT.Sigmoid)
@@ -288,27 +298,10 @@ def tile_grouptorchgru_t_e_kernel(
         make_identity(nc, ident_f32[:])
         ident_bf = const.tile([P, P], BF16)
         make_identity(nc, ident_bf[:])
-
-        w_planes = const.tile([P, UNITS, GATES * HID], U8, align_bytes=64)
-        nc.vector.memset(w_planes[:].bitcast(I32), 0)
-        bias_rows = const.tile([P, P], BF16)
-        nc.vector.memset(bias_rows[:], 0.0)
-
-        load(0)
         whh_rows = const.tile([P, UNITS * GATES, HID], BF16)
-        nc.sync.dma_start(out=whh_rows[:], in_=w_hh.rearrange("u (g m) k -> m (u g) k", m=P))
-        n_bias = UNITS * GATES
-        nc.sync.dma_start(out=bias_rows[0:n_bias, :], in_=b_ih.rearrange("u (g h) -> (u g) h", h=HID))
-        nc.sync.dma_start(
-            out=bias_rows[n_bias : 2 * n_bias, :], in_=b_hh.rearrange("u (g h) -> (u g) h", h=HID)
-        )
-        for quadrant in range(4):
-            nc.sync.dma_start(
-                out=w_planes[32 * quadrant : 32 * quadrant + 4, :, :].bitcast(I32),
-                in_=w_ih_scales[:, 4 * quadrant : 4 * quadrant + 4, :]
-                .rearrange("u q n -> q u n")
-                .bitcast(I32),
-            )
+        nc.gpsimd.dma_start(out=bias_rows[0:UNITS, :], in_=b_ih)
+        nc.gpsimd.dma_start(out=bias_rows[UNITS : 2 * UNITS, :], in_=b_hh)
+
         w_words = const.tile([P, UNITS, GATES * HID], U32, align_bytes=64)
 
         def load_words(u):
@@ -317,11 +310,23 @@ def tile_grouptorchgru_t_e_kernel(
                 in_=w_ih_words[u].rearrange("p n t -> p (n t)").bitcast(I32),
             )
 
+        load_inputs(0)
+        for quadrant in range(4):
+            nc.sync.dma_start(
+                out=w_planes[32 * quadrant : 32 * quadrant + 4, :, :].bitcast(I32),
+                in_=w_ih_scales[:, 4 * quadrant : 4 * quadrant + 4, :]
+                .rearrange("u q n -> q u n")
+                .bitcast(I32),
+            )
+        load_hidden(0)
+        nc.sync.dma_start(out=whh_rows[:], in_=w_hh.rearrange("u (g m) k -> m (u g) k", m=P))
         load_words(0)
-        load(1)
+        load_inputs(1)
+        load_hidden(1)
+        load_words(1)
         load(2)
-        for u in range(1, UNITS):
-            load_words(u)
+        load_words(2)
+        load_words(3)
         load(3)
 
         transpose_inputs(0, 0)
@@ -333,24 +338,31 @@ def tile_grouptorchgru_t_e_kernel(
         quantise(0)
 
         whh_t = const.tile([P, UNITS * GATES, P], BF16)
-        bias_ih = const.tile([P, n_bias], F32)
-        bias_hh = const.tile([P, n_bias], F32)
-        bias_sum = const.tile([P, n_bias], F32)
-        bias_neg = const.tile([P, n_bias], F32)
+        bias_ih = const.tile([P, GATES, UNITS], F32)
+        bias_hh = const.tile([P, GATES, UNITS], F32)
+        bias_sum = const.tile([P, GATES, UNITS], F32)
+        bias_neg = const.tile([P, GATES, UNITS], F32)
 
-        bias_ps = psum.tile([P, P], BF16, tag="bank")
-        nc.tensor.transpose(bias_ps[:], bias_rows[:], ident_bf[:])
-        nc.vector.tensor_copy(out=bias_ih[:], in_=bias_ps[:, 0:n_bias])
-        nc.vector.tensor_copy(out=bias_hh[:], in_=bias_ps[:, n_bias : 2 * n_bias])
+        bias_ps = psum.tile([P, GATES, P], BF16, tag="bank")
+        for gate in range(GATES):
+            nc.tensor.transpose(
+                bias_ps[:, gate, :], bias_rows[:, gate * HID : (gate + 1) * HID], ident_bf[:]
+            )
+        nc.vector.tensor_copy(out=bias_ih[:], in_=bias_ps[:, :, 0:UNITS])
+        nc.vector.tensor_copy(out=bias_hh[:], in_=bias_ps[:, :, UNITS : 2 * UNITS])
         nc.vector.tensor_tensor(out=bias_sum[:], in0=bias_ih[:], in1=bias_hh[:], op=ALU.add)
         nc.vector.tensor_scalar_mul(out=bias_neg[:], in0=bias_sum[:], scalar1=-1.0)
-        for u in range(UNITS):
+
+        def transpose_weights(u):
             whh_ps = psum.tile([P, GATES, P], BF16, tag="bank")
             for gate in range(GATES):
                 nc.tensor.transpose(
                     whh_ps[:, gate, :], whh_rows[:, u * GATES + gate, :], ident_bf[:]
                 )
             nc.scalar.copy(out=whh_t[:, u * GATES : (u + 1) * GATES, :], in_=whh_ps[:])
+
+        for u in range(UNITS):
+            transpose_weights(u)
 
         for i in range(N_CHUNKS + BEHIND_OUT):
             cand, ahead = i - BEHIND_CAND, i + AHEAD_IN

@@ -18,7 +18,8 @@ GATES = 3
 RESET, UPDATE, NEW = 0, 1, 2
 CHUNK = 512
 SHORT = CHUNK // 2
-LAST = (BATCH // CHUNK) * UNITS
+BLOCKS = BATCH // CHUNK
+LAST = BLOCKS * UNITS
 N_CHUNKS = LAST + 1
 WORDS = K_IN // 2
 
@@ -40,7 +41,7 @@ def tile_grouptorchgru_t_e_kernel(
         ctx.enter_context(tc.manual_schedule())
         const = ctx.enter_context(tc.tile_pool(name="const", bufs=1))
         x_pool = ctx.enter_context(tc.tile_pool(name="x", bufs=4))
-        hid_pool = ctx.enter_context(tc.tile_pool(name="hid", bufs=4))
+        hid_pool = ctx.enter_context(tc.tile_pool(name="hid", bufs=9))
         mx_pool = ctx.enter_context(tc.tile_pool(name="mx", bufs=5))
         ht_pool = ctx.enter_context(tc.tile_pool(name="ht", bufs=6))
         work = ctx.enter_context(tc.tile_pool(name="work", bufs=2))
@@ -54,7 +55,7 @@ def tile_grouptorchgru_t_e_kernel(
         new_of, diff_of, blend_of, back_of = {}, {}, {}, {}
 
         def unit(c):
-            return c % UNITS
+            return (c % LAST) // BLOCKS
 
         def rows(c):
             return SHORT if c in (0, LAST) else CHUNK
@@ -63,7 +64,7 @@ def tile_grouptorchgru_t_e_kernel(
             return rows(c) // P
 
         def batch_rows(c):
-            first = SHORT if c == LAST else (c // UNITS) * CHUNK
+            first = SHORT if c == LAST else (c % BLOCKS) * CHUNK
             return slice(first, first + rows(c))
 
         def column(bias, c, gate):
@@ -79,40 +80,31 @@ def tile_grouptorchgru_t_e_kernel(
             x_of[c] = x
 
         def load_hidden(c):
-            if c in (0, LAST):
-                units = slice(0, 1)
-            elif c == 1:
-                units = slice(1, UNITS)
-            elif unit(c) == 0:
-                units = slice(0, UNITS)
-            else:
-                units = slice(0, 0)
-            count = units.stop - units.start
-            if count > 0:
-                hid = hid_pool.tile([P, groups(c), count, HID], BF16)
-                nc.sync.dma_start(
-                    out=hid[:],
-                    in_=hidden[batch_rows(c), units, :].rearrange("(p j) u h -> p j u h", j=groups(c)),
-                )
-                for k in range(count):
-                    hid_of[c + k] = hid[:, :, k, :]
+            hid = hid_pool.tile([P, groups(c), HID], BF16)
+            nc.sync.dma_start(
+                out=hid[:],
+                in_=hidden[batch_rows(c), unit(c), :].rearrange("(p j) h -> p j h", j=groups(c)),
+            )
+            hid_of[c] = hid
 
         def load(c):
             load_inputs(c)
             load_hidden(c)
 
-        def transpose_inputs(c, half):
+        def transpose_inputs(c, half, steps=range(4)):
             n = groups(c) // 2
-            xt = psum.tile([P, 2, n * P], F32, tag="bank")
+            if 0 in steps:
+                xt = psum.tile([P, 2, n * P], F32, tag="bank")
+                xt_of[c, half] = xt
             x_words = x_of[c][:].bitcast(F32)
-            for jj in range(n):
-                for w in range(2):
+            for step in steps:
+                jj, w = divmod(step, 2)
+                if jj < n:
                     nc.tensor.transpose(
-                        xt[:, w, jj * P : (jj + 1) * P],
+                        xt_of[c, half][:, w, jj * P : (jj + 1) * P],
                         x_words[:, n * half + jj, w:WORDS:2],
                         ident_f32[:],
                     )
-            xt_of[c, half] = xt
 
         def copy_inputs(c, half, copy):
             if half == 0:
@@ -145,13 +137,16 @@ def tile_grouptorchgru_t_e_kernel(
             codes_of[c] = codes
             planes_of[c] = planes
 
-        def matmul_hidden(c, gate):
-            gh = psum.tile([P, rows(c)], F32, tag="bank")
+        def matmul_hidden(c, gate, half=None):
+            if half in (None, 0):
+                gh = psum.tile([P, rows(c)], F32, tag="bank")
+                gh_of[c, gate] = gh
+            n = rows(c) // 2
+            cols = slice(0, rows(c)) if half is None else slice(half * n, (half + 1) * n)
             nc.tensor.matmul(
-                out=gh[:], lhsT=whh_t[:, unit(c) * GATES + gate, :], rhs=ht_of[c][:],
-                start=True, stop=True,
+                out=gh_of[c, gate][:, cols], lhsT=whh_t[:, unit(c) * GATES + gate, :],
+                rhs=ht_of[c][:, cols], start=True, stop=True,
             )
-            gh_of[c, gate] = gh
 
         def matmul_inputs(c, gate):
             cols = slice(gate * HID, (gate + 1) * HID)
@@ -188,18 +183,24 @@ def tile_grouptorchgru_t_e_kernel(
             nc.scalar.copy(out=xz[:], in_=xz_ps_of[c][:])
             xz_of[c] = xz
 
-        def sum_update(c):
-            z_ps = psum.tile([P, rows(c)], F32, tag="bank")
+        def open_update(c, half):
+            if half == 0:
+                z_ps = psum.tile([P, rows(c)], F32, tag="bank")
+                z_ps_of[c] = z_ps
+            n = rows(c) // 2
+            cols = slice(half * n, (half + 1) * n)
             nc.tensor.matmul(
-                out=z_ps[:], lhsT=whh_t[:, unit(c) * GATES + UPDATE, :], rhs=ht_of[c][:],
-                start=True, stop=False,
+                out=z_ps_of[c][:, cols], lhsT=whh_t[:, unit(c) * GATES + UPDATE, :],
+                rhs=ht_of[c][:, cols], start=True, stop=False,
             )
-            for j in range(groups(c)):
+
+        def add_update(c, half):
+            n = groups(c) // 2
+            for j in range(half * n, (half + 1) * n):
                 nc.tensor.matmul(
-                    out=z_ps[:, j * P : (j + 1) * P], lhsT=xz_of[c][:, j, :], rhs=ident_f32[:],
-                    is_transpose=True, start=False, stop=(j == groups(c) - 1),
+                    out=z_ps_of[c][:, j * P : (j + 1) * P], lhsT=xz_of[c][:, j, :], rhs=ident_f32[:],
+                    is_transpose=True, start=False, stop=(j == (half + 1) * n - 1),
                 )
-            z_ps_of[c] = z_ps
 
         def sigmoid_update(c):
             keep = late.tile([P, rows(c)], F32)
@@ -276,7 +277,7 @@ def tile_grouptorchgru_t_e_kernel(
 
         def store(c):
             result = late.tile([P, groups(c), HID], F32)
-            nc.vector.tensor_tensor(out=result[:], in0=back_of[c][:], in1=hid_of[c], op=ALU.add)
+            nc.vector.tensor_tensor(out=result[:], in0=back_of[c][:], in1=hid_of[c][:], op=ALU.add)
             nc.sync.dma_start(
                 out=out[batch_rows(c), unit(c), :].rearrange("(p j) h -> p j h", j=groups(c)),
                 in_=result[:],
@@ -287,9 +288,9 @@ def tile_grouptorchgru_t_e_kernel(
                 stage(c, *args)
 
         w_planes = const.tile([P, UNITS, GATES * HID], U8, align_bytes=64)
-        nc.vector.memset(w_planes[:].bitcast(I32), 0)
         bias_rows = const.tile([P, GATES * HID], BF16)
         nc.vector.memset(bias_rows[:], 0.0)
+        nc.vector.memset(w_planes[:].bitcast(I32), 0)
         warm = const.tile([P, 1], F32)
         nc.vector.memset(warm[:], 0.0)
         nc.scalar.activation(out=warm[:], in_=warm[:], func=ACT.Sigmoid)
@@ -299,8 +300,6 @@ def tile_grouptorchgru_t_e_kernel(
         ident_bf = const.tile([P, P], BF16)
         make_identity(nc, ident_bf[:])
         whh_rows = const.tile([P, UNITS * GATES, HID], BF16)
-        nc.gpsimd.dma_start(out=bias_rows[0:UNITS, :], in_=b_ih)
-        nc.gpsimd.dma_start(out=bias_rows[UNITS : 2 * UNITS, :], in_=b_hh)
 
         w_words = const.tile([P, UNITS, GATES * HID], U32, align_bytes=64)
 
@@ -310,24 +309,34 @@ def tile_grouptorchgru_t_e_kernel(
                 in_=w_ih_words[u].rearrange("p n t -> p (n t)").bitcast(I32),
             )
 
-        load_inputs(0)
-        for quadrant in range(4):
+        def load_scales(units):
+            for quadrant in range(4):
+                nc.sync.dma_start(
+                    out=w_planes[32 * quadrant : 32 * quadrant + 4, units, :].bitcast(I32),
+                    in_=w_ih_scales[units, 4 * quadrant : 4 * quadrant + 4, :]
+                    .rearrange("u q n -> q u n")
+                    .bitcast(I32),
+                )
+
+        def load_w_hh(u):
             nc.sync.dma_start(
-                out=w_planes[32 * quadrant : 32 * quadrant + 4, :, :].bitcast(I32),
-                in_=w_ih_scales[:, 4 * quadrant : 4 * quadrant + 4, :]
-                .rearrange("u q n -> q u n")
-                .bitcast(I32),
+                out=whh_rows[:, u * GATES : (u + 1) * GATES, :],
+                in_=w_hh[u].rearrange("(g m) k -> m g k", m=P),
             )
+
+        load_inputs(0)
+        nc.sync.dma_start(out=bias_rows[0:UNITS, :], in_=b_ih)
+        nc.sync.dma_start(out=bias_rows[UNITS : 2 * UNITS, :], in_=b_hh)
         load_hidden(0)
-        nc.sync.dma_start(out=whh_rows[:], in_=w_hh.rearrange("u (g m) k -> m (u g) k", m=P))
-        load_words(0)
+        load_w_hh(0)
         load_inputs(1)
+        load_words(0)
+        load_scales(slice(0, UNITS))
+        load_inputs(2)
         load_hidden(1)
-        load_words(1)
-        load(2)
-        load_words(2)
-        load_words(3)
-        load(3)
+        load_hidden(2)
+        load_inputs(3)
+        load_hidden(3)
 
         transpose_inputs(0, 0)
         copy_inputs(0, 0, nc.scalar.copy)
@@ -343,6 +352,16 @@ def tile_grouptorchgru_t_e_kernel(
         bias_sum = const.tile([P, GATES, UNITS], F32)
         bias_neg = const.tile([P, GATES, UNITS], F32)
 
+        def transpose_weights(u):
+            whh_ps = psum.tile([P, GATES, P], BF16, tag="bank")
+            for gate in range(GATES):
+                nc.tensor.transpose(
+                    whh_ps[:, gate, :], whh_rows[:, u * GATES + gate, :], ident_bf[:]
+                )
+            nc.scalar.copy(out=whh_t[:, u * GATES : (u + 1) * GATES, :], in_=whh_ps[:])
+
+        transpose_weights(0)
+
         bias_ps = psum.tile([P, GATES, P], BF16, tag="bank")
         for gate in range(GATES):
             nc.tensor.transpose(
@@ -353,21 +372,14 @@ def tile_grouptorchgru_t_e_kernel(
         nc.vector.tensor_tensor(out=bias_sum[:], in0=bias_ih[:], in1=bias_hh[:], op=ALU.add)
         nc.vector.tensor_scalar_mul(out=bias_neg[:], in0=bias_sum[:], scalar1=-1.0)
 
-        def transpose_weights(u):
-            whh_ps = psum.tile([P, GATES, P], BF16, tag="bank")
-            for gate in range(GATES):
-                nc.tensor.transpose(
-                    whh_ps[:, gate, :], whh_rows[:, u * GATES + gate, :], ident_bf[:]
-                )
-            nc.scalar.copy(out=whh_t[:, u * GATES : (u + 1) * GATES, :], in_=whh_ps[:])
-
-        for u in range(UNITS):
-            transpose_weights(u)
-
+        for half in range(2):
+            matmul_hidden(0, RESET, half)
         for i in range(N_CHUNKS + BEHIND_OUT):
             cand, ahead = i - BEHIND_CAND, i + AHEAD_IN
             run(load, i + AHEAD_LOAD)
-            run(matmul_hidden, i, RESET)
+            if 0 < i < UNITS:
+                load_w_hh(i)
+                load_words(i)
             run(copy_hidden_reset, i)
             run(candidate, i - BEHIND_BLEND)
             if on_gpsimd(i - BEHIND_BLEND):
@@ -379,10 +391,6 @@ def tile_grouptorchgru_t_e_kernel(
             run(matmul_inputs_update, i)
             run(copy_inputs_update, i)
             run(matmul_inputs, cand, NEW)
-            run(matmul_hidden, cand, NEW)
-            run(gate_hidden, cand)
-            if not on_gpsimd(i - BEHIND_BLEND):
-                run(difference, i - BEHIND_BLEND)
             if i == 0:
                 for half, copy in ((0, nc.scalar.copy), (1, nc.vector.tensor_copy)):
                     transpose_inputs(1, half)
@@ -390,18 +398,45 @@ def tile_grouptorchgru_t_e_kernel(
                 transpose_hidden(1)
                 copy_hidden(1, nc.scalar.copy)
                 quantise(1)
-            run(transpose_inputs, ahead, 0)
-            run(copy_inputs, ahead, 0, nc.scalar.copy)
-            run(sigmoid_reset, i)
+            run(matmul_hidden, cand, NEW, 0)
+            run(transpose_inputs, ahead, 0, (0,))
+            run(transpose_inputs, ahead, 0, (1,))
+            run(matmul_hidden, cand, NEW, 1)
+            run(gate_hidden, cand)
+            run(transpose_inputs, ahead, 0, (2,))
+            run(transpose_inputs, ahead, 0, (3,))
+            if i % 2 == 1:
+                run(copy_inputs, ahead, 0, nc.scalar.copy)
+            if i % 2 == 0:
+                run(copy_inputs, ahead, 0, nc.scalar.copy)
             run(transpose_hidden, ahead)
-            run(copy_hidden, ahead, nc.vector.tensor_copy)
+            if i % 2 == 1:
+                run(copy_hidden, ahead, nc.scalar.copy)
+            run(sigmoid_reset, i)
+            if i % 2 == 0:
+                run(copy_hidden, ahead, nc.vector.tensor_copy)
             run(sum_candidate, cand)
-            run(sum_update, cand)
+            if not on_gpsimd(i - BEHIND_BLEND):
+                run(difference, i - BEHIND_BLEND)
+            if 2 <= i < 1 + UNITS:
+                transpose_weights(i - 1)
+            run(open_update, cand, 0)
+            run(transpose_inputs, ahead, 1, (0,))
+            run(transpose_inputs, ahead, 1, (1,))
+            run(add_update, cand, 0)
+            run(open_update, cand, 1)
+            run(transpose_inputs, ahead, 1, (2,))
+            run(add_update, cand, 1)
             run(sigmoid_update, cand)
-            run(transpose_inputs, ahead, 1)
-            run(copy_inputs, ahead, 1, nc.vector.tensor_copy)
+            run(matmul_hidden, i + 1, RESET, 0)
+            run(transpose_inputs, ahead, 1, (3,))
+            if i % 2 == 1:
+                run(copy_inputs, ahead, 1, nc.vector.tensor_copy)
+            if i % 2 == 0:
+                run(copy_inputs, ahead, 1, nc.vector.tensor_copy)
             if not on_gpsimd(i - BEHIND_BLEND):
                 run(blend, i - BEHIND_BLEND)
             run(transpose_out, i - BEHIND_OUT)
             run(store, i - BEHIND_OUT)
             run(quantise, ahead)
+            run(matmul_hidden, i + 1, RESET, 1)

@@ -91,20 +91,18 @@ def tile_grouptorchgru_t_e_kernel(
             load_inputs(c)
             load_hidden(c)
 
-        def transpose_inputs(c, half, steps=range(4)):
+        def transpose_inputs(c, half):
             n = groups(c) // 2
-            if 0 in steps:
-                xt = psum.tile([P, 2, n * P], F32, tag="bank")
-                xt_of[c, half] = xt
+            xt = psum.tile([P, 2, n * P], F32, tag="bank")
             x_words = x_of[c][:].bitcast(F32)
-            for step in steps:
-                jj, w = divmod(step, 2)
-                if jj < n:
+            for jj in range(n):
+                for w in range(2):
                     nc.tensor.transpose(
-                        xt_of[c, half][:, w, jj * P : (jj + 1) * P],
+                        xt[:, w, jj * P : (jj + 1) * P],
                         x_words[:, n * half + jj, w:WORDS:2],
                         ident_f32[:],
                     )
+            xt_of[c, half] = xt
 
         def copy_inputs(c, half, copy):
             if half == 0:
@@ -137,16 +135,13 @@ def tile_grouptorchgru_t_e_kernel(
             codes_of[c] = codes
             planes_of[c] = planes
 
-        def matmul_hidden(c, gate, half=None):
-            if half in (None, 0):
-                gh = psum.tile([P, rows(c)], F32, tag="bank")
-                gh_of[c, gate] = gh
-            n = rows(c) // 2
-            cols = slice(0, rows(c)) if half is None else slice(half * n, (half + 1) * n)
+        def matmul_hidden(c, gate):
+            gh = psum.tile([P, rows(c)], F32, tag="bank")
             nc.tensor.matmul(
-                out=gh_of[c, gate][:, cols], lhsT=whh_t[:, unit(c) * GATES + gate, :],
-                rhs=ht_of[c][:, cols], start=True, stop=True,
+                out=gh[:], lhsT=whh_t[:, unit(c) * GATES + gate, :], rhs=ht_of[c][:],
+                start=True, stop=True,
             )
+            gh_of[c, gate] = gh
 
         def matmul_inputs(c, gate):
             cols = slice(gate * HID, (gate + 1) * HID)
@@ -183,23 +178,19 @@ def tile_grouptorchgru_t_e_kernel(
             nc.scalar.copy(out=xz[:], in_=xz_ps_of[c][:])
             xz_of[c] = xz
 
-        def open_update(c, half):
-            if half == 0:
-                z_ps = psum.tile([P, rows(c)], F32, tag="bank")
-                z_ps_of[c] = z_ps
-            n = rows(c) // 2
-            cols = slice(half * n, (half + 1) * n)
+        def open_update(c):
+            z_ps = psum.tile([P, rows(c)], F32, tag="bank")
             nc.tensor.matmul(
-                out=z_ps_of[c][:, cols], lhsT=whh_t[:, unit(c) * GATES + UPDATE, :],
-                rhs=ht_of[c][:, cols], start=True, stop=False,
+                out=z_ps[:], lhsT=whh_t[:, unit(c) * GATES + UPDATE, :], rhs=ht_of[c][:],
+                start=True, stop=False,
             )
+            z_ps_of[c] = z_ps
 
-        def add_update(c, half):
-            n = groups(c) // 2
-            for j in range(half * n, (half + 1) * n):
+        def add_update(c):
+            for j in range(groups(c)):
                 nc.tensor.matmul(
                     out=z_ps_of[c][:, j * P : (j + 1) * P], lhsT=xz_of[c][:, j, :], rhs=ident_f32[:],
-                    is_transpose=True, start=False, stop=(j == (half + 1) * n - 1),
+                    is_transpose=True, start=False, stop=(j == groups(c) - 1),
                 )
 
         def sigmoid_update(c):
@@ -372,25 +363,32 @@ def tile_grouptorchgru_t_e_kernel(
         nc.vector.tensor_tensor(out=bias_sum[:], in0=bias_ih[:], in1=bias_hh[:], op=ALU.add)
         nc.vector.tensor_scalar_mul(out=bias_neg[:], in0=bias_sum[:], scalar1=-1.0)
 
-        for half in range(2):
-            matmul_hidden(0, RESET, half)
         for i in range(N_CHUNKS + BEHIND_OUT):
             cand, ahead = i - BEHIND_CAND, i + AHEAD_IN
             run(load, i + AHEAD_LOAD)
             if 0 < i < UNITS:
                 load_w_hh(i)
                 load_words(i)
-            run(copy_hidden_reset, i)
             run(candidate, i - BEHIND_BLEND)
             if on_gpsimd(i - BEHIND_BLEND):
                 run(difference, i - BEHIND_BLEND)
             if on_gpsimd(i - BEHIND_BLEND):
                 run(blend, i - BEHIND_BLEND)
+            run(matmul_hidden, i, RESET)
+            run(copy_hidden_reset, i)
+            run(matmul_hidden, cand, NEW)
+            run(gate_hidden, cand)
             run(matmul_inputs, i, RESET)
             run(sum_reset, i)
             run(matmul_inputs_update, i)
             run(copy_inputs_update, i)
             run(matmul_inputs, cand, NEW)
+            run(sum_candidate, cand)
+            if not on_gpsimd(i - BEHIND_BLEND):
+                run(difference, i - BEHIND_BLEND)
+            if not on_gpsimd(i - BEHIND_BLEND):
+                run(blend, i - BEHIND_BLEND)
+            run(open_update, cand)
             if i == 0:
                 for half, copy in ((0, nc.scalar.copy), (1, nc.vector.tensor_copy)):
                     transpose_inputs(1, half)
@@ -398,45 +396,17 @@ def tile_grouptorchgru_t_e_kernel(
                 transpose_hidden(1)
                 copy_hidden(1, nc.scalar.copy)
                 quantise(1)
-            run(matmul_hidden, cand, NEW, 0)
-            run(transpose_inputs, ahead, 0, (0,))
-            run(transpose_inputs, ahead, 0, (1,))
-            run(matmul_hidden, cand, NEW, 1)
-            run(gate_hidden, cand)
-            run(transpose_inputs, ahead, 0, (2,))
-            run(transpose_inputs, ahead, 0, (3,))
-            if i % 2 == 1:
-                run(copy_inputs, ahead, 0, nc.scalar.copy)
-            if i % 2 == 0:
-                run(copy_inputs, ahead, 0, nc.scalar.copy)
-            run(transpose_hidden, ahead)
-            if i % 2 == 1:
-                run(copy_hidden, ahead, nc.scalar.copy)
-            run(sigmoid_reset, i)
-            if i % 2 == 0:
-                run(copy_hidden, ahead, nc.vector.tensor_copy)
-            run(sum_candidate, cand)
-            if not on_gpsimd(i - BEHIND_BLEND):
-                run(difference, i - BEHIND_BLEND)
-            if 2 <= i < 1 + UNITS:
-                transpose_weights(i - 1)
-            run(open_update, cand, 0)
-            run(transpose_inputs, ahead, 1, (0,))
-            run(transpose_inputs, ahead, 1, (1,))
-            run(add_update, cand, 0)
-            run(open_update, cand, 1)
-            run(transpose_inputs, ahead, 1, (2,))
-            run(add_update, cand, 1)
+            run(transpose_inputs, ahead, 0)
+            run(copy_inputs, ahead, 0, nc.scalar.copy)
+            run(add_update, cand)
             run(sigmoid_update, cand)
-            run(matmul_hidden, i + 1, RESET, 0)
-            run(transpose_inputs, ahead, 1, (3,))
-            if i % 2 == 1:
-                run(copy_inputs, ahead, 1, nc.vector.tensor_copy)
-            if i % 2 == 0:
-                run(copy_inputs, ahead, 1, nc.vector.tensor_copy)
-            if not on_gpsimd(i - BEHIND_BLEND):
-                run(blend, i - BEHIND_BLEND)
+            run(sigmoid_reset, i)
+            run(transpose_inputs, ahead, 1)
+            run(copy_inputs, ahead, 1, nc.vector.tensor_copy)
             run(transpose_out, i - BEHIND_OUT)
             run(store, i - BEHIND_OUT)
             run(quantise, ahead)
-            run(matmul_hidden, i + 1, RESET, 1)
+            if 2 <= i < 1 + UNITS:
+                transpose_weights(i - 1)
+            run(transpose_hidden, ahead)
+            run(copy_hidden, ahead, nc.vector.tensor_copy)

from contextlib import ExitStack

import concourse.mybir as mybir
from concourse.masks import make_identity

F32 = mybir.dt.float32
BF16 = mybir.dt.bfloat16
I32 = mybir.dt.int32
U32 = mybir.dt.uint32
U8 = mybir.dt.uint8
FP8X4 = mybir.dt.float8_e4m3fn_x4
ACT = mybir.ActivationFunctionType
ALU = mybir.AluOpType

BATCH, UNITS, K_IN, HID = 4096, 4, 512, 128
P = 128
GATES = 3
RESET, UPDATE, NEW = 0, 1, 2
CHUNK = 512
SHORT = CHUNK // 2
BLOCKS = BATCH // CHUNK
LAST = BLOCKS * UNITS
N_CHUNKS = LAST + 1
WORDS = K_IN // 2

AHEAD_LOAD = 4
AHEAD_IN = 2
BEHIND_CAND = 1
BEHIND_BLEND = 2
BEHIND_OUT = 3
BLEND_ON_VECTOR = 2

FLOPS = 2 * BATCH * UNITS * (K_IN + HID) * GATES * HID


def tile_grouptorchgru_t_e_kernel(
    tc, inputs, hidden, w_ih_words, w_ih_scales, w_hh, b_ih, b_hh, out
):
    nc = tc.nc
    with ExitStack() as ctx:
        ctx.enter_context(tc.manual_schedule())
        const = ctx.enter_context(tc.tile_pool(name="const", bufs=1))
        x_pool = ctx.enter_context(tc.tile_pool(name="x", bufs=4))
        hid_pool = ctx.enter_context(tc.tile_pool(name="hid", bufs=9))
        mx_pool = ctx.enter_context(tc.tile_pool(name="mx", bufs=5))
        ht_pool = ctx.enter_context(tc.tile_pool(name="ht", bufs=6))
        work = ctx.enter_context(tc.tile_pool(name="work", bufs=2))
        late = ctx.enter_context(tc.tile_pool(name="late", bufs=4))
        mid = ctx.enter_context(tc.tile_pool(name="mid", bufs=3))
        psum = ctx.enter_context(tc.psum_pool(name="psum", bufs=8))

        x_of, hid_of, xt_of, grouped_of, codes_of, planes_of = {}, {}, {}, {}, {}, {}
        ht_ps_of, ht_of, gh_of, gx_of, xz_ps_of, xz_of, z_ps_of = {}, {}, {}, {}, {}, {}, {}
        pre_of, reset_of, keep_of, gated_of, cand_of = {}, {}, {}, {}, {}
        new_of, diff_of, blend_of, back_of = {}, {}, {}, {}

        def unit(c):
            return (c % LAST) // BLOCKS

        def rows(c):
            return SHORT if c in (0, LAST) else CHUNK

        def groups(c):
            return rows(c) // P

        def batch_rows(c):
            first = SHORT if c == LAST else (c % BLOCKS) * CHUNK
            return slice(first, first + rows(c))

        def column(bias, c, gate):
            u = unit(c)
            return bias[:, gate, u : u + 1]

        def load_inputs(c):
            x = x_pool.tile([P, groups(c), K_IN], BF16)
            nc.sync.dma_start(
                out=x[:],
                in_=inputs[batch_rows(c), unit(c), :].rearrange("(p j) k -> p j k", j=groups(c)),
            )
            x_of[c] = x

        def load_hidden(c):
            hid = hid_pool.tile([P, groups(c), HID], BF16)
            nc.sync.dma_start(
                out=hid[:],
                in_=hidden[batch_rows(c), unit(c), :].rearrange("(p j) h -> p j h", j=groups(c)),
            )
            hid_of[c] = hid

        def load(c):
            load_inputs(c)
            load_hidden(c)

        def transpose_inputs(c, half):
            n = groups(c) // 2
            xt = psum.tile([P, 2, n * P], F32, tag="bank")
            x_words = x_of[c][:].bitcast(F32)
            for jj in range(n):
                for w in range(2):
                    nc.tensor.transpose(
                        xt[:, w, jj * P : (jj + 1) * P],
                        x_words[:, n * half + jj, w:WORDS:2],
                        ident_f32[:],
                    )
            xt_of[c, half] = xt

        def copy_inputs(c, half, copy):
            if half == 0:
                grouped = work.tile([P, rows(c) * 4], BF16, align_bytes=64)
                grouped_of[c] = grouped
            grouped_words = grouped_of[c][:].bitcast(F32).rearrange("p (r w) -> p r w", w=2)
            n = rows(c) // 2
            copy(
                out=grouped_words[:, half * n : (half + 1) * n, :],
                in_=xt_of[c, half][:].rearrange("p w r -> p r w"),
            )

        def transpose_hidden(c):
            ht_ps = psum.tile([P, rows(c)], BF16, tag="bank")
            for j in range(groups(c)):
                nc.tensor.transpose(ht_ps[:, j * P : (j + 1) * P], hid_of[c][:, j, :], ident_bf[:])
            ht_ps_of[c] = ht_ps

        def copy_hidden(c, copy):
            ht = ht_pool.tile([P, rows(c)], BF16)
            copy(out=ht[:], in_=ht_ps_of[c][:])
            ht_of[c] = ht

        def quantise(c):
            codes = mx_pool.tile([P, rows(c)], U32, align_bytes=64)
            planes = mx_pool.tile([P, rows(c)], U8, align_bytes=64)
            nc.vector.quantize_mx(
                out=codes[:].bitcast(FP8X4), scales=planes[:], in_=grouped_of[c][:]
            )
            codes_of[c] = codes
            planes_of[c] = planes

        def matmul_hidden(c, gate):
            gh = psum.tile([P, rows(c)], F32, tag="bank")
            nc.tensor.matmul(
                out=gh[:], lhsT=whh_t[:, unit(c) * GATES + gate, :], rhs=ht_of[c][:],
                start=True, stop=True,
            )
            gh_of[c, gate] = gh

        def matmul_inputs(c, gate):
            cols = slice(gate * HID, (gate + 1) * HID)
            gx = psum.tile([P, rows(c)], F32, tag="bank")
            nc.tensor.matmul_mx(
                out=gx[:],
                lhsT=w_words[:, unit(c), cols].bitcast(FP8X4),
                lhsT_scale=w_planes[:, unit(c), cols],
                rhs=codes_of[c][:].bitcast(FP8X4),
                rhs_scale=planes_of[c][:],
                start=True,
                stop=True,
            )
            gx_of[c, gate] = gx

        def matmul_inputs_update(c):
            cols = slice(UPDATE * HID, (UPDATE + 1) * HID)
            xz_ps = psum.tile([P, groups(c), HID], F32, tag="bank")
            for j in range(groups(c)):
                part = slice(j * P, (j + 1) * P)
                nc.tensor.matmul_mx(
                    out=xz_ps[:, j, :],
                    lhsT=codes_of[c][:, part].bitcast(FP8X4),
                    lhsT_scale=planes_of[c][:, part],
                    rhs=w_words[:, unit(c), cols].bitcast(FP8X4),
                    rhs_scale=w_planes[:, unit(c), cols],
                    start=True,
                    stop=True,
                )
            xz_ps_of[c] = xz_ps

        def copy_inputs_update(c):
            xz = mid.tile([P, groups(c), HID], F32)
            nc.scalar.copy(out=xz[:], in_=xz_ps_of[c][:])
            xz_of[c] = xz

        def open_update(c):
            z_ps = psum.tile([P, rows(c)], F32, tag="bank")
            nc.tensor.matmul(
                out=z_ps[:], lhsT=whh_t[:, unit(c) * GATES + UPDATE, :], rhs=ht_of[c][:],
                start=True, stop=False,
            )
            z_ps_of[c] = z_ps

        def add_update(c):
            for j in range(groups(c)):
                nc.tensor.matmul(
                    out=z_ps_of[c][:, j * P : (j + 1) * P], lhsT=xz_of[c][:, j, :], rhs=ident_f32[:],
                    is_transpose=True, start=False, stop=(j == groups(c) - 1),
                )

        def sigmoid_update(c):
            keep = late.tile([P, rows(c)], F32)
            nc.scalar.activation(
                out=keep[:], in_=z_ps_of[c][:], func=ACT.Sigmoid,
                bias=column(bias_neg, c, UPDATE), scale=-1.0,
            )
            keep_of[c] = keep

        def copy_hidden_reset(c):
            pre = work.tile([P, rows(c)], F32)
            nc.scalar.activation(
                out=pre[:], in_=gh_of[c, RESET][:], func=ACT.Identity,
                bias=column(bias_sum, c, RESET), scale=1.0,
            )
            pre_of[c] = pre

        def sum_reset(c):
            nc.vector.tensor_tensor(
                out=pre_of[c][:], in0=pre_of[c][:], in1=gx_of[c, RESET][:], op=ALU.add
            )

        def sigmoid_reset(c):
            reset = mid.tile([P, rows(c)], F32)
            nc.scalar.activation(out=reset[:], in_=pre_of[c][:], func=ACT.Sigmoid)
            reset_of[c] = reset

        def gate_hidden(c):
            gated = work.tile([P, rows(c)], F32)
            nc.vector.scalar_tensor_tensor(
                out=gated[:], in0=gh_of[c, NEW][:], scalar=column(bias_hh, c, NEW),
                in1=reset_of[c][:], op0=ALU.add, op1=ALU.mult,
            )
            gated_of[c] = gated

        def sum_candidate(c):
            cand = work.tile([P, rows(c)], F32)
            nc.vector.tensor_tensor(
                out=cand[:], in0=gated_of[c][:], in1=gx_of[c, NEW][:], op=ALU.add
            )
            cand_of[c] = cand

        def on_gpsimd(c):
            return c < N_CHUNKS - BLEND_ON_VECTOR

        def blend_engine(c):
            return nc.gpsimd if on_gpsimd(c) else nc.vector

        def candidate(c):
            new = work.tile([P, rows(c)], F32)
            nc.scalar.activation(
                out=new[:], in_=cand_of[c][:], func=ACT.Tanh,
                bias=column(bias_ih, c, NEW), scale=1.0,
            )
            new_of[c] = new

        def difference(c):
            diff = work.tile([P, rows(c)], F32)
            blend_engine(c).tensor_tensor(
                out=diff[:], in0=new_of[c][:], in1=ht_of[c][:], op=ALU.subtract
            )
            diff_of[c] = diff

        def blend(c):
            mixed = late.tile([P, rows(c)], F32)
            blend_engine(c).tensor_tensor(out=mixed[:], in0=keep_of[c][:], in1=diff_of[c][:], op=ALU.mult)
            blend_of[c] = mixed

        def transpose_out(c):
            back = psum.tile([P, groups(c), HID], F32, tag="bank")
            for j in range(groups(c)):
                nc.tensor.transpose(back[:, j, :], blend_of[c][:, j * P : (j + 1) * P], ident_f32[:])
            back_of[c] = back

        def store(c):
            result = late.tile([P, groups(c), HID], F32)
            nc.vector.tensor_tensor(out=result[:], in0=back_of[c][:], in1=hid_of[c][:], op=ALU.add)
            nc.sync.dma_start(
                out=out[batch_rows(c), unit(c), :].rearrange("(p j) h -> p j h", j=groups(c)),
                in_=result[:],
            )

        def run(stage, c, *args):
            if 0 <= c < N_CHUNKS:
                stage(c, *args)

        w_planes = const.tile([P, UNITS, GATES * HID], U8, align_bytes=64)
        bias_rows = const.tile([P, GATES * HID], BF16)
        nc.vector.memset(bias_rows[:], 0.0)
        nc.vector.memset(w_planes[:].bitcast(I32), 0)
        warm = const.tile([P, 1], F32)
        nc.vector.memset(warm[:], 0.0)
        nc.scalar.activation(out=warm[:], in_=warm[:], func=ACT.Sigmoid)

        ident_f32 = const.tile([P, P], F32)
        make_identity(nc, ident_f32[:])
        ident_bf = const.tile([P, P], BF16)
        make_identity(nc, ident_bf[:])
        whh_rows = const.tile([P, UNITS * GATES, HID], BF16)

        w_words = const.tile([P, UNITS, GATES * HID], U32, align_bytes=64)

        def load_words(u):
            nc.sync.dma_start(
                out=w_words[:, u, :].bitcast(I32),
                in_=w_ih_words[u].rearrange("p n t -> p (n t)").bitcast(I32),
            )

        def load_scales(units):
            for quadrant in range(4):
                nc.sync.dma_start(
                    out=w_planes[32 * quadrant : 32 * quadrant + 4, units, :].bitcast(I32),
                    in_=w_ih_scales[units, 4 * quadrant : 4 * quadrant + 4, :]
                    .rearrange("u q n -> q u n")
                    .bitcast(I32),
                )

        def load_w_hh(u):
            nc.sync.dma_start(
                out=whh_rows[:, u * GATES : (u + 1) * GATES, :],
                in_=w_hh[u].rearrange("(g m) k -> m g k", m=P),
            )

        load_inputs(0)
        nc.sync.dma_start(out=bias_rows[0:UNITS, :], in_=b_ih)
        nc.sync.dma_start(out=bias_rows[UNITS : 2 * UNITS, :], in_=b_hh)
        load_hidden(0)
        load_w_hh(0)
        load_inputs(1)
        load_words(0)
        load_scales(slice(0, UNITS))
        load_inputs(2)
        load_hidden(1)
        load_hidden(2)
        load_inputs(3)
        load_hidden(3)

        transpose_inputs(0, 0)
        copy_inputs(0, 0, nc.scalar.copy)
        transpose_inputs(0, 1)
        copy_inputs(0, 1, nc.vector.tensor_copy)
        transpose_hidden(0)
        copy_hidden(0, nc.scalar.copy)
        quantise(0)

        whh_t = const.tile([P, UNITS * GATES, P], BF16)
        bias_ih = const.tile([P, GATES, UNITS], F32)
        bias_hh = const.tile([P, GATES, UNITS], F32)
        bias_sum = const.tile([P, GATES, UNITS], F32)
        bias_neg = const.tile([P, GATES, UNITS], F32)

        def transpose_weights(u):
            whh_ps = psum.tile([P, GATES, P], BF16, tag="bank")
            for gate in range(GATES):
                nc.tensor.transpose(
                    whh_ps[:, gate, :], whh_rows[:, u * GATES + gate, :], ident_bf[:]
                )
            nc.scalar.copy(out=whh_t[:, u * GATES : (u + 1) * GATES, :], in_=whh_ps[:])

        transpose_weights(0)

        bias_ps = psum.tile([P, GATES, P], BF16, tag="bank")
        for gate in range(GATES):
            nc.tensor.transpose(
                bias_ps[:, gate, :], bias_rows[:, gate * HID : (gate + 1) * HID], ident_bf[:]
            )
        nc.vector.tensor_copy(out=bias_ih[:], in_=bias_ps[:, :, 0:UNITS])
        nc.vector.tensor_copy(out=bias_hh[:], in_=bias_ps[:, :, UNITS : 2 * UNITS])
        nc.vector.tensor_tensor(out=bias_sum[:], in0=bias_ih[:], in1=bias_hh[:], op=ALU.add)
        nc.vector.tensor_scalar_mul(out=bias_neg[:], in0=bias_sum[:], scalar1=-1.0)

        for i in range(N_CHUNKS + BEHIND_OUT):
            cand, ahead = i - BEHIND_CAND, i + AHEAD_IN
            run(load, i + AHEAD_LOAD)
            if 0 < i < UNITS:
                load_w_hh(i)
                load_words(i)
            run(candidate, i - BEHIND_BLEND)
            if on_gpsimd(i - BEHIND_BLEND):
                run(difference, i - BEHIND_BLEND)
            if on_gpsimd(i - BEHIND_BLEND):
                run(blend, i - BEHIND_BLEND)
            run(matmul_hidden, i, RESET)
            run(copy_hidden_reset, i)
            run(matmul_hidden, cand, NEW)
            run(gate_hidden, cand)
            run(matmul_inputs, i, RESET)
            run(sum_reset, i)
            run(matmul_inputs_update, i)
            run(copy_inputs_update, i)
            run(matmul_inputs, cand, NEW)
            run(sum_candidate, cand)
            if not on_gpsimd(i - BEHIND_BLEND):
                run(difference, i - BEHIND_BLEND)
            if not on_gpsimd(i - BEHIND_BLEND):
                run(blend, i - BEHIND_BLEND)
            run(open_update, cand)
            if i == 0:
                for half, copy in ((0, nc.scalar.copy), (1, nc.vector.tensor_copy)):
                    transpose_inputs(1, half)
                    copy_inputs(1, half, copy)
                transpose_hidden(1)
                copy_hidden(1, nc.scalar.copy)
                quantise(1)
            run(transpose_inputs, ahead, 0)
            run(copy_inputs, ahead, 0, nc.scalar.copy)
            run(add_update, cand)
            run(sigmoid_update, cand)
            run(sigmoid_reset, i)
            run(transpose_inputs, ahead, 1)
            run(copy_inputs, ahead, 1, nc.vector.tensor_copy)
            run(transpose_out, i - BEHIND_OUT)
            run(store, i - BEHIND_OUT)
            run(quantise, ahead)
            if 2 <= i < 1 + UNITS:
                transpose_weights(i - 1)
            run(transpose_hidden, ahead)
            run(copy_hidden, ahead, nc.vector.tensor_copy)
